import numpy as np
import ml_dtypes


def mxq(x, axis, fmt="e4m3"):
    dtype, down = {"e4m3": (ml_dtypes.float8_e4m3fn, 7), "e5m2": (ml_dtypes.float8_e5m2, 14)}[fmt]
    v = np.moveaxis(np.asarray(x, np.float32).astype(ml_dtypes.bfloat16).astype(np.float64), axis, -1)
    blocks = v.reshape(v.shape[:-1] + (-1, 32))
    amax = np.abs(blocks).max(-1, keepdims=True)
    byte = np.maximum(np.where(amax > 0, np.frexp(amax)[1] - 1 + 127, 0) - down, 1)
    scale = np.exp2(byte - 127.0)
    codes = (blocks / scale).astype(np.float32).astype(dtype).astype(np.float64)
    return np.moveaxis((codes * scale).reshape(v.shape), -1, axis)


WIDE = False


def mx_kscale(k):
    if not WIDE:
        return np.ones(k)
    levels = np.array([10, -10, 5, -5, 0])
    a = np.random.permutation(np.resize(levels, k // 512 * 4)).reshape(k // 512, 4)
    idx = np.arange(k)
    return np.exp2(a[idx // 512, idx % 128 // 32])


BF16 = ml_dtypes.bfloat16


def bf(x):
    return np.asarray(x, np.float32).astype(BF16)


def f64(x):
    return np.asarray(x).astype(np.float64)


E2M1 = np.array([0.0, 0.5, 1.0, 1.5, 2.0, 3.0, 4.0, 6.0, -0.0, -0.5, -1.0, -1.5, -2.0, -3.0, -4.0, -6.0])


def pack_weight(w, fmt):
    k, n = w.shape
    w = f64(bf(w)).reshape(k // 32, 32, n)
    amax = np.abs(w).max(1)
    if fmt == "e4m3":
        byte = np.frexp(amax)[1] - 1 + 127 - 7
    else:
        mant, ex = np.frexp(amax / 6.0)
        byte = np.where(mant > 0.5, ex, ex - 1) + 127
    byte = np.clip(np.where(amax > 0, byte, 1), 1, 254)
    scaled = (w * np.exp2(127.0 - byte)[:, None, :]).reshape(k, n).astype(np.float32)
    by_word = np.ascontiguousarray(scaled.reshape(k // 512, 128, 4, n).transpose(0, 1, 3, 2))
    if fmt == "e4m3":
        words = by_word.astype(ml_dtypes.float8_e4m3fn).view(np.uint8)
    else:
        c = by_word.astype(ml_dtypes.float4_e2m1fn).view(np.uint8) & 0xF
        words = c[..., 0::2] | (c[..., 1::2] << 4)
    return np.ascontiguousarray(words), np.ascontiguousarray(byte.astype(np.uint8).reshape(k // 512, 16, n))


def unpack_weight(words, scales, fmt):
    g, p, n, _ = words.shape
    if fmt == "e4m3":
        vals = np.ascontiguousarray(words).view(ml_dtypes.float8_e4m3fn).astype(np.float64)
    else:
        nib = np.empty((g, p, n, 4), np.uint8)
        nib[..., 0::2] = words & 0xF
        nib[..., 1::2] = words >> 4
        vals = E2M1[nib]
    vals = vals * np.repeat(np.exp2(scales.astype(np.float64) - 127.0), 8, axis=1)[..., None]
    return vals.transpose(0, 1, 3, 2).reshape(g * 512, n)


N, D, H = 512, 16384, 512
H2 = H + H
LN_EPS = 1e-5
ERF_TERMS = 120
FMT = "e4m3"


def erf(x):
    a = np.clip(x, -6.0, 6.0)
    term = a
    total = a
    for n in range(1, ERF_TERMS):
        term = term * (2.0 * a * a / (2.0 * n + 1.0))
        total = total + term
    return 2.0 / np.sqrt(np.pi) * np.exp(-a * a) * total


def gelu(v):
    return 0.5 * v * (1.0 + erf(v / np.sqrt(2.0)))


def layernorm(x, g, b):
    m = x.mean(-1, keepdims=True)
    v = np.square(x - m).mean(-1, keepdims=True)
    return (x - m) / np.sqrt(v + LN_EPS) * g + b


def setup_inputs():
    s, t = mx_kscale(D), mx_kscale(H2)
    z = bf(np.random.standard_normal((N, D)) * s)
    attention_out = bf(np.random.standard_normal((N, H)) * t[H:])
    Wz_words, Wz_scales = pack_weight(np.ascontiguousarray((np.random.standard_normal((H, D)) / np.sqrt(D) / s).T), FMT)
    bz = bf(0.1 * np.random.standard_normal(H))
    gz = bf((1.0 + 0.1 * np.random.standard_normal(H)) * t[:H])
    bz_ln = bf(0.1 * np.random.standard_normal(H) * t[:H])
    w1_deq_words, w1_deq_scales = pack_weight(np.ascontiguousarray((np.random.standard_normal((H, H2)) / np.sqrt(H2) / t).T), FMT)
    b1 = bf(0.1 * np.random.standard_normal(H))
    g1 = bf(1.0 + 0.1 * np.random.standard_normal(H))
    b1_ln = bf(0.1 * np.random.standard_normal(H))
    return {
        "z": z,
        "attention_out": attention_out,
        "Wz_words": Wz_words,
        "Wz_scales": Wz_scales,
        "bz": bz,
        "gz": gz,
        "bz_ln": bz_ln,
        "w1_deq_words": w1_deq_words,
        "w1_deq_scales": w1_deq_scales,
        "b1": b1,
        "g1": g1,
        "b1_ln": b1_ln,
    }


def reference(z, attention_out, Wz_words, Wz_scales, bz, gz, bz_ln, w1_deq_words, w1_deq_scales, b1, g1, b1_ln):
    z_proj = layernorm((mxq(f64(z), 1, "e4m3") @ unpack_weight(Wz_words, Wz_scales, FMT)) + f64(bz), f64(gz), f64(bz_ln))
    combined = np.concatenate([z_proj, f64(attention_out)], axis=-1)
    y = (mxq(combined, 1, "e4m3") @ unpack_weight(w1_deq_words, w1_deq_scales, FMT)) + f64(b1)
    return gelu(layernorm(y, f64(g1), f64(b1_ln)))

@@ -1,0 +1,403 @@
+from contextlib import ExitStack
+
+import concourse.mybir as mybir
+from concourse.masks import make_identity
+
+F32 = mybir.dt.float32
+BF16 = mybir.dt.bfloat16
+I32 = mybir.dt.int32
+U32 = mybir.dt.uint32
+U8 = mybir.dt.uint8
+FP8X4 = mybir.dt.float8_e4m3fn_x4
+ALU = mybir.AluOpType
+ACT = mybir.ActivationFunctionType
+
+P = 128
+PACK = 4
+K_PASS = P * PACK
+TOKENS = 512
+D_IN = 16384
+HID = 512
+LN_EPS = 1e-5
+
+TOKEN_TILES = TOKENS // P
+CHUNK_GROUPS = 8
+CHUNK_K = CHUNK_GROUPS * K_PASS
+CHUNKS = D_IN // CHUNK_K
+QUANT_GROUPS = 4
+Z_BUFS = 5
+
+FLOPS = 2 * TOKENS * D_IN * HID + 2 * TOKENS * (2 * HID) * HID
+
+EARLY_CHUNKS = CHUNKS // 2
+ROUNDS = [(c, m) for c in range(EARLY_CHUNKS) for m in range(TOKEN_TILES)] + [
+    (c, m) for m in range(TOKEN_TILES) for c in range(EARLY_CHUNKS, CHUNKS)
+]
+N_ROUNDS = len(ROUNDS)
+
+
+def tile_synapsemodel_pa_k_kernel(
+    tc,
+    z,
+    attention_out,
+    Wz_words,
+    Wz_scales,
+    bz,
+    gz,
+    bz_ln,
+    w1_deq_words,
+    w1_deq_scales,
+    b1,
+    g1,
+    b1_ln,
+    out,
+):
+    nc = tc.nc
+
+    first_round_of_chunk = {}
+    last_round_of_tile = {}
+    for k, (c, m) in enumerate(ROUNDS):
+        if c not in first_round_of_chunk:
+            first_round_of_chunk[c] = k
+        last_round_of_tile[m] = k
+    tile_finished_in = {k: m for m, k in last_round_of_tile.items()}
+
+    with ExitStack() as ctx:
+        const = ctx.enter_context(tc.tile_pool(name="const", bufs=1))
+        z_pool = ctx.enter_context(tc.tile_pool(name="z_pool", bufs=Z_BUFS))
+        sorted_pool = ctx.enter_context(tc.tile_pool(name="sorted_pool", bufs=3))
+        grouped_pool = ctx.enter_context(tc.tile_pool(name="grouped_pool", bufs=2))
+        codes_pool = ctx.enter_context(tc.tile_pool(name="codes_pool", bufs=3))
+        post = ctx.enter_context(tc.tile_pool(name="post", bufs=2))
+        stat = ctx.enter_context(tc.tile_pool(name="stat", bufs=2))
+        psum = ctx.enter_context(tc.psum_pool(name="psum", bufs=1))
+        ctx.enter_context(tc.manual_schedule())
+
+        sum_bank = ["sum_bank%d" % m for m in range(TOKEN_TILES)]
+        turn_bank = ["turn_bank%d" % b for b in range(CHUNK_GROUPS // 2)]
+
+        vectors = (bz, b1, g1, b1_ln, gz, bz_ln)
+        vector_rows = const.tile([P, len(vectors), HID], BF16, name="vector_rows")
+        nc.vector.memset(vector_rows[:].rearrange("p v h -> p (v h)").bitcast(I32), 0)
+        for v, vector in enumerate(vectors):
+            nc.scalar.dma_start(out=vector_rows[0:1, v, :], in_=vector.unsqueeze(0))
+        ones = const.tile([P, P], BF16, name="ones")
+        nc.vector.memset(ones[:], 1.0)
+        neg_half = const.tile([P, 1], F32, name="neg_half")
+        nc.vector.memset(neg_half[:], -0.5)
+
+        wz_planes = const.tile([P, CHUNK_GROUPS, HID], U8, name="wz_planes", align_bytes=64)
+        nc.vector.memset(wz_planes[:].rearrange("p g n -> p (g n)").bitcast(I32), 0)
+        w1_planes = const.tile([P, 2, HID], U8, name="w1_planes", align_bytes=64)
+        nc.vector.memset(w1_planes[:].rearrange("p g n -> p (g n)").bitcast(I32), 0)
+
+        warm = const.tile([P, 1], F32, name="warm")
+        nc.vector.memset(warm[:], 0.0)
+        warm_out = const.tile([P, 1], F32, name="warm_out")
+        nc.scalar.activation(out=warm_out[:], in_=warm[:], func=ACT.Gelu)
+
+        ident_f32 = const.tile([P, P], F32, name="ident_f32")
+        make_identity(nc, ident_f32[:])
+        ident_bf16 = const.tile([P, P], BF16, name="ident_bf16")
+        make_identity(nc, ident_bf16[:])
+
+        att_raw = const.tile([P, TOKEN_TILES * HID], BF16, name="att_raw")
+        nc.sync.dma_start(
+            out=att_raw[:].rearrange("p (m k) -> p m k", m=TOKEN_TILES),
+            in_=attention_out.rearrange("(m p) k -> p m k", p=P),
+        )
+
+        z_raw = {}
+        wz_words = {}
+        w1_words = const.tile([P, 2, PACK * HID], U8, name="w1_words", align_bytes=64)
+
+        def load_scale_rows(planes, offset, scales):
+            rows = scales.rearrange("g (q r) n -> r q g n", r=4)
+            for r in range(4):
+                nc.sync.dma_start(
+                    out=planes[offset + r : P : 32, :, :].bitcast(I32), in_=rows[r].bitcast(I32)
+                )
+
+        def load_words(words, packed, groups):
+            nc.sync.dma_start(
+                out=words[:, groups, :].bitcast(I32),
+                in_=packed[groups].rearrange("g p n t -> p g (n t)").bitcast(I32),
+            )
+
+        def load_chunk_weights(c):
+            chunk = slice(c * CHUNK_GROUPS, (c + 1) * CHUNK_GROUPS)
+            load_scale_rows(wz_planes, PACK * c, Wz_scales[chunk])
+            wz_words[c] = const.tile(
+                [P, CHUNK_GROUPS, PACK * HID], U8, name="wz_words%d" % c, align_bytes=64
+            )
+            for half in range(2):
+                load_words(
+                    wz_words[c],
+                    Wz_words[chunk],
+                    slice(half * QUANT_GROUPS, (half + 1) * QUANT_GROUPS),
+                )
+
+        def load_round(k):
+            if k >= N_ROUNDS:
+                return
+            c, m = ROUNDS[k]
+            z_raw[k] = z_pool.tile([P, CHUNK_K], BF16, name="z_raw")
+            nc.sync.dma_start(
+                out=z_raw[k][:], in_=z[m * P : (m + 1) * P, c * CHUNK_K : (c + 1) * CHUNK_K]
+            )
+            for chunk, first in first_round_of_chunk.items():
+                if first == k - 1:
+                    load_chunk_weights(chunk)
+                    if chunk == CHUNKS - 1:
+                        load_scale_rows(w1_planes, 0, w1_deq_scales)
+                        load_words(w1_words, w1_deq_words, slice(0, 2))
+
+        def sort_words(raw, units):
+            in_runs = sorted_pool.tile([P, units, 2, P], F32, name="in_runs")
+            nc.vector.tensor_copy(
+                out=in_runs[:],
+                in_=raw[:].bitcast(F32).rearrange("p (a q u) -> p a u q", a=units, u=2),
+            )
+            return in_runs
+
+        def transpose_units(in_runs, units, banks):
+            turned = []
+            for b in range(units // 2):
+                bank = psum.tile([P, 2, 2, P], F32, name="turned", tag=banks[b])
+                for a in range(2):
+                    for u in range(2):
+                        nc.tensor.transpose(bank[:, a, u, :], in_runs[:, 2 * b + a, u, :], ident_f32[:])
+                turned.append(bank)
+            return turned
+
+        def interleave(turned, units):
+            grouped = grouped_pool.tile([P, units * P * PACK], BF16, name="grouped", align_bytes=64)
+            pairs = grouped[:].bitcast(F32).rearrange("p (a m u) -> p a m u", a=units, u=2)
+            for b, bank in enumerate(turned):
+                nc.scalar.copy(
+                    out=pairs[:, 2 * b : 2 * b + 2], in_=bank[:].rearrange("p a u m -> p a m u")
+                )
+            return grouped
+
+        def quantise(grouped, codes, planes, units):
+            for first in range(0, units, QUANT_GROUPS):
+                cols = slice(first * P, (first + QUANT_GROUPS) * P)
+                nc.vector.quantize_mx(
+                    out=codes[:, cols].bitcast(FP8X4),
+                    scales=planes[:, cols],
+                    in_=grouped[:, first * P * PACK : (first + QUANT_GROUPS) * P * PACK],
+                )
+
+        z_runs = {}
+        z_turned = {}
+        z_grouped = {}
+        z_codes = {}
+        z_planes = {}
+        sums = {}
+        passes_done = {m: 0 for m in range(TOKEN_TILES)}
+
+        def sort_round(k):
+            z_runs[k] = sort_words(z_raw[k], CHUNK_GROUPS)
+
+        def transpose_round(k):
+            z_turned[k] = transpose_units(z_runs[k], CHUNK_GROUPS, turn_bank)
+            z_grouped[k] = interleave(z_turned[k], CHUNK_GROUPS)
+
+        def quantise_round(k):
+            z_codes[k] = codes_pool.tile([P, CHUNK_GROUPS * P], U32, name="z_codes", align_bytes=64)
+            z_planes[k] = codes_pool.tile([P, CHUNK_GROUPS * P], U8, name="z_planes", align_bytes=64)
+            quantise(z_grouped[k], z_codes[k], z_planes[k], CHUNK_GROUPS)
+
+        def multiply_round(k):
+            c, m = ROUNDS[k]
+            if passes_done[m] == 0:
+                sums[m] = psum.tile([P, HID], F32, name="sums", tag=sum_bank[m])
+            for g in range(CHUNK_GROUPS):
+                tokens = slice(g * P, (g + 1) * P)
+                nc.tensor.matmul_mx(
+                    out=sums[m][:],
+                    lhsT=z_codes[k][:, tokens].bitcast(FP8X4),
+                    lhsT_scale=z_planes[k][:, tokens],
+                    rhs=wz_words[c][:, g, :].bitcast(FP8X4),
+                    rhs_scale=wz_planes[PACK * c : P, g, :],
+                    start=(passes_done[m] == 0),
+                    stop=(passes_done[m] == D_IN // K_PASS - 1),
+                )
+                passes_done[m] += 1
+
+        def norm_head(sums_in, bias, gain, by_word_position):
+            x = post.tile([P, HID], F32, name="x")
+            total = stat.tile([P, 1], F32, name="total")
+            nc.vector.scalar_tensor_tensor(
+                out=x[:], in0=sums_in[:], scalar=1.0, in1=bias, op0=ALU.mult, op1=ALU.add, accum_out=total[:]
+            )
+            neg_mean = stat.tile([P, 1], F32, name="neg_mean")
+            nc.vector.tensor_scalar(
+                out=neg_mean[:], in0=total[:], scalar1=-1.0 / HID, scalar2=None, op0=ALU.mult
+            )
+            squares = post.tile([P, HID], BF16, name="squares")
+            sum_sq = stat.tile([P, 1], F32, name="sum_sq")
+            nc.scalar.activation(
+                out=squares[:], in_=x[:], func=ACT.Square, bias=neg_mean[:], scale=1.0, accum_out=sum_sq[:]
+            )
+            var_eps = stat.tile([P, 1], F32, name="var_eps")
+            nc.gpsimd.tensor_scalar(
+                out=var_eps[:], in0=sum_sq[:], scalar1=1.0 / HID, scalar2=LN_EPS, op0=ALU.mult, op1=ALU.add
+            )
+            rstd = stat.tile([P, 1], F32, name="rstd")
+            nc.gpsimd.tensor_tensor(out=rstd[:], in0=var_eps[:], in1=neg_half[:], op=ALU.pow)
+            centred = post.tile([P, HID], F32, name="centred")
+            if by_word_position:
+                x_view = x[:].rearrange("p (q t) -> p t q", t=PACK)
+                shape = "p (t q) -> p t q"
+            else:
+                x_view = x[:].rearrange("p (t q) -> p t q", t=PACK)
+                shape = "p (t q) -> p t q"
+            nc.vector.scalar_tensor_tensor(
+                out=centred[:].rearrange(shape, t=PACK),
+                in0=x_view,
+                scalar=neg_mean[:],
+                in1=gain.rearrange(shape, t=PACK),
+                op0=ALU.add,
+                op1=ALU.mult,
+            )
+            return centred, rstd
+
+        def norm_tail(centred, rstd, shift, result):
+            nc.vector.scalar_tensor_tensor(
+                out=result, in0=centred[:], scalar=rstd[:], in1=shift, op0=ALU.mult, op1=ALU.add
+            )
+
+        for k in range(Z_BUFS):
+            load_round(k)
+
+        spread = const.tile([P, len(vectors), HID], BF16, name="spread")
+        for pair in range(len(vectors) // 2):
+            both = psum.tile([P, 2, HID], BF16, name="both", tag=sum_bank[pair])
+            for v in range(2):
+                nc.tensor.matmul(
+                    out=both[:, v, :], lhsT=ones[:], rhs=vector_rows[:, 2 * pair + v, :], start=True, stop=True
+                )
+            if pair < 2:
+                nc.scalar.copy(out=spread[:, 2 * pair : 2 * pair + 2, :], in_=both[:])
+            else:
+                nc.scalar.copy(
+                    out=spread[:, 2 * pair : 2 * pair + 2, :].rearrange("p v (t q) -> p v t q", t=PACK),
+                    in_=both[:].rearrange("p v (q t) -> p v t q", t=PACK),
+                )
+        bz_all, b1_all, g1_all, b1_ln_all, gz_all, bz_ln_all = [spread[:, v, :] for v in range(len(vectors))]
+
+        att_runs = sort_words(att_raw, TOKEN_TILES)
+        att_turned = transpose_units(att_runs, TOKEN_TILES, [sum_bank[3], sum_bank[0]])
+        att_grouped = interleave(att_turned, TOKEN_TILES)
+        att_codes = const.tile([P, TOKENS], U32, name="att_codes", align_bytes=64)
+        att_planes = const.tile([P, TOKENS], U8, name="att_planes", align_bytes=64)
+
+        sort_round(0)
+        load_round(Z_BUFS)
+        sort_round(1)
+        load_round(Z_BUFS + 1)
+        transpose_round(0)
+        quantise(att_grouped, att_codes, att_planes, TOKEN_TILES)
+        quantise_round(0)
+
+        centred_1 = {}
+        rstd_1 = {}
+        z_proj = {}
+        zp_grouped = {}
+        zp_codes = {}
+        zp_planes = {}
+        y_sums = {}
+        centred_2 = {}
+        rstd_2 = {}
+        normed = {}
+
+        def first_norm_head(m):
+            centred_1[m], rstd_1[m] = norm_head(sums[m], bz_all, gz_all, True)
+
+        def first_norm_tail(m):
+            z_proj[m] = post.tile([P, PACK, P], BF16, name="z_proj")
+            norm_tail(centred_1[m], rstd_1[m], bz_ln_all, z_proj[m][:].rearrange("p t q -> p (t q)"))
+
+        def transpose_z_proj(m):
+            turned = psum.tile([P, PACK, P], BF16, name="zp_turned", tag=sum_bank[m])
+            for t in range(PACK):
+                nc.tensor.transpose(turned[:, t, :], z_proj[m][:, t, :], ident_bf16[:])
+            zp_grouped[m] = post.tile([P, P, PACK], BF16, name="zp_grouped", align_bytes=64)
+            nc.scalar.copy(out=zp_grouped[m][:], in_=turned[:].rearrange("p t m -> p m t"))
+
+        def quantise_z_proj(m):
+            zp_codes[m] = post.tile([P, P], U32, name="zp_codes", align_bytes=64)
+            zp_planes[m] = post.tile([P, P], U8, name="zp_planes", align_bytes=64)
+            nc.vector.quantize_mx(
+                out=zp_codes[m][:].bitcast(FP8X4),
+                scales=zp_planes[m][:],
+                in_=zp_grouped[m][:].rearrange("p m t -> p (m t)"),
+            )
+
+        def second_matmul(m):
+            tokens = slice(m * P, (m + 1) * P)
+            y_sums[m] = psum.tile([P, HID], F32, name="y_sums", tag=sum_bank[m])
+            nc.tensor.matmul_mx(
+                out=y_sums[m][:],
+                lhsT=att_codes[:, tokens].bitcast(FP8X4),
+                lhsT_scale=att_planes[:, tokens],
+                rhs=w1_words[:, 1, :].bitcast(FP8X4),
+                rhs_scale=w1_planes[:, 1, :],
+                start=True,
+                stop=False,
+            )
+            nc.tensor.matmul_mx(
+                out=y_sums[m][:],
+                lhsT=zp_codes[m][:].bitcast(FP8X4),
+                lhsT_scale=zp_planes[m][:],
+                rhs=w1_words[:, 0, :].bitcast(FP8X4),
+                rhs_scale=w1_planes[:, 0, :],
+                start=False,
+                stop=True,
+            )
+
+        def second_norm_head(m):
+            centred_2[m], rstd_2[m] = norm_head(y_sums[m], b1_all, g1_all, False)
+
+        def second_norm_tail(m):
+            normed[m] = post.tile([P, HID], F32, name="normed")
+            norm_tail(centred_2[m], rstd_2[m], b1_ln_all, normed[m][:])
+
+        def gelu_and_store(m):
+            result = post.tile([P, HID], F32, name="result")
+            nc.scalar.activation(out=result[:], in_=normed[m][:], func=ACT.Gelu)
+            nc.sync.dma_start(out=out[m * P : (m + 1) * P, :], in_=result[:])
+
+        SECOND_STAGE_STEPS = 3
+        for k in range(N_ROUNDS + SECOND_STAGE_STEPS + 1):
+            ended_now = tile_finished_in.get(k)
+            ended_1_ago = tile_finished_in.get(k - 1)
+            ended_2_ago = tile_finished_in.get(k - 2)
+            ended_3_ago = tile_finished_in.get(k - 3)
+
+            if k + 2 < N_ROUNDS:
+                sort_round(k + 2)
+                load_round(k + 2 + Z_BUFS)
+            if ended_1_ago is not None:
+                first_norm_tail(ended_1_ago)
+            if ended_2_ago is not None:
+                quantise_z_proj(ended_2_ago)
+            if ended_3_ago is not None:
+                second_norm_tail(ended_3_ago)
+            if k + 1 < N_ROUNDS:
+                transpose_round(k + 1)
+            if ended_3_ago is not None:
+                gelu_and_store(ended_3_ago)
+            if ended_2_ago is not None:
+                second_matmul(ended_2_ago)
+            if k < N_ROUNDS:
+                multiply_round(k)
+            if ended_1_ago is not None:
+                transpose_z_proj(ended_1_ago)
+            if k + 1 < N_ROUNDS:
+                quantise_round(k + 1)
+            if ended_2_ago is not None:
+                second_norm_head(ended_2_ago)
+            if ended_now is not None:
+                first_norm_head(ended_now)

@@ -25,7 +25,7 @@ CHUNK_GROUPS = 8
 CHUNK_K = CHUNK_GROUPS * K_PASS
 CHUNKS = D_IN // CHUNK_K
 QUANT_GROUPS = 4
-Z_BUFS = 5
+Z_BUFS = 6
 
 FLOPS = 2 * TOKENS * D_IN * HID + 2 * TOKENS * (2 * HID) * HID
 
@@ -65,7 +65,6 @@ def tile_synapsemodel_pa_k_kernel(
     with ExitStack() as ctx:
         const = ctx.enter_context(tc.tile_pool(name="const", bufs=1))
         z_pool = ctx.enter_context(tc.tile_pool(name="z_pool", bufs=Z_BUFS))
-        sorted_pool = ctx.enter_context(tc.tile_pool(name="sorted_pool", bufs=3))
         grouped_pool = ctx.enter_context(tc.tile_pool(name="grouped_pool", bufs=2))
         codes_pool = ctx.enter_context(tc.tile_pool(name="codes_pool", bufs=3))
         post = ctx.enter_context(tc.tile_pool(name="post", bufs=2))
@@ -152,21 +151,14 @@ def tile_synapsemodel_pa_k_kernel(
                         load_scale_rows(w1_planes, 0, w1_deq_scales)
                         load_words(w1_words, w1_deq_words, slice(0, 2))
 
-        def sort_words(raw, units):
-            in_runs = sorted_pool.tile([P, units, 2, P], F32, name="in_runs")
-            nc.vector.tensor_copy(
-                out=in_runs[:],
-                in_=raw[:].bitcast(F32).rearrange("p (a q u) -> p a u q", a=units, u=2),
-            )
-            return in_runs
-
-        def transpose_units(in_runs, units, banks):
+        def transpose_units(raw, units, banks):
+            words = raw[:].bitcast(F32).rearrange("p (a q u) -> p a u q", a=units, u=2)
             turned = []
             for b in range(units // 2):
                 bank = psum.tile([P, 2, 2, P], F32, name="turned", tag=banks[b])
                 for a in range(2):
                     for u in range(2):
-                        nc.tensor.transpose(bank[:, a, u, :], in_runs[:, 2 * b + a, u, :], ident_f32[:])
+                        nc.tensor.transpose(bank[:, a, u, :], words[:, 2 * b + a, u, :], ident_f32[:])
                 turned.append(bank)
             return turned
 
@@ -188,7 +180,6 @@ def tile_synapsemodel_pa_k_kernel(
                     in_=grouped[:, first * P * PACK : (first + QUANT_GROUPS) * P * PACK],
                 )
 
-        z_runs = {}
         z_turned = {}
         z_grouped = {}
         z_codes = {}
@@ -196,12 +187,10 @@ def tile_synapsemodel_pa_k_kernel(
         sums = {}
         passes_done = {m: 0 for m in range(TOKEN_TILES)}
 
-        def sort_round(k):
-            z_runs[k] = sort_words(z_raw[k], CHUNK_GROUPS)
-
         def transpose_round(k):
-            z_turned[k] = transpose_units(z_runs[k], CHUNK_GROUPS, turn_bank)
+            z_turned[k] = transpose_units(z_raw[k], CHUNK_GROUPS, turn_bank)
             z_grouped[k] = interleave(z_turned[k], CHUNK_GROUPS)
+            load_round(k + Z_BUFS)
 
         def quantise_round(k):
             z_codes[k] = codes_pool.tile([P, CHUNK_GROUPS * P], U32, name="z_codes", align_bytes=64)
@@ -287,16 +276,11 @@ def tile_synapsemodel_pa_k_kernel(
                 )
         bz_all, b1_all, g1_all, b1_ln_all, gz_all, bz_ln_all = [spread[:, v, :] for v in range(len(vectors))]
 
-        att_runs = sort_words(att_raw, TOKEN_TILES)
-        att_turned = transpose_units(att_runs, TOKEN_TILES, [sum_bank[3], sum_bank[0]])
+        att_turned = transpose_units(att_raw, TOKEN_TILES, [sum_bank[3], sum_bank[0]])
         att_grouped = interleave(att_turned, TOKEN_TILES)
         att_codes = const.tile([P, TOKENS], U32, name="att_codes", align_bytes=64)
         att_planes = const.tile([P, TOKENS], U8, name="att_planes", align_bytes=64)
 
-        sort_round(0)
-        load_round(Z_BUFS)
-        sort_round(1)
-        load_round(Z_BUFS + 1)
         transpose_round(0)
         quantise(att_grouped, att_codes, att_planes, TOKEN_TILES)
         quantise_round(0)
@@ -376,9 +360,6 @@ def tile_synapsemodel_pa_k_kernel(
             ended_2_ago = tile_finished_in.get(k - 2)
             ended_3_ago = tile_finished_in.get(k - 3)
 
-            if k + 2 < N_ROUNDS:
-                sort_round(k + 2)
-                load_round(k + 2 + Z_BUFS)
             if ended_1_ago is not None:
                 first_norm_tail(ended_1_ago)
             if ended_2_ago is not None:

@@ -25,7 +25,7 @@ CHUNK_GROUPS = 8
 CHUNK_K = CHUNK_GROUPS * K_PASS
 CHUNKS = D_IN // CHUNK_K
 QUANT_GROUPS = 4
-Z_BUFS = 6
+Z_BUFS = 5
 
 FLOPS = 2 * TOKENS * D_IN * HID + 2 * TOKENS * (2 * HID) * HID
 
@@ -65,6 +65,7 @@ def tile_synapsemodel_pa_k_kernel(
     with ExitStack() as ctx:
         const = ctx.enter_context(tc.tile_pool(name="const", bufs=1))
         z_pool = ctx.enter_context(tc.tile_pool(name="z_pool", bufs=Z_BUFS))
+        sorted_pool = ctx.enter_context(tc.tile_pool(name="sorted_pool", bufs=3))
         grouped_pool = ctx.enter_context(tc.tile_pool(name="grouped_pool", bufs=2))
         codes_pool = ctx.enter_context(tc.tile_pool(name="codes_pool", bufs=3))
         post = ctx.enter_context(tc.tile_pool(name="post", bufs=2))
@@ -75,7 +76,7 @@ def tile_synapsemodel_pa_k_kernel(
         sum_bank = ["sum_bank%d" % m for m in range(TOKEN_TILES)]
         turn_bank = ["turn_bank%d" % b for b in range(CHUNK_GROUPS // 2)]
 
-        vectors = (bz, b1, g1, b1_ln, gz, bz_ln)
+        vectors = (bz, gz, bz_ln, b1, g1, b1_ln)
         vector_rows = const.tile([P, len(vectors), HID], BF16, name="vector_rows")
         nc.vector.memset(vector_rows[:].rearrange("p v h -> p (v h)").bitcast(I32), 0)
         for v, vector in enumerate(vectors):
@@ -85,37 +86,39 @@ def tile_synapsemodel_pa_k_kernel(
         neg_half = const.tile([P, 1], F32, name="neg_half")
         nc.vector.memset(neg_half[:], -0.5)
 
-        wz_planes = const.tile([P, CHUNK_GROUPS, HID], U8, name="wz_planes", align_bytes=64)
-        nc.vector.memset(wz_planes[:].rearrange("p g n -> p (g n)").bitcast(I32), 0)
-        w1_planes = const.tile([P, 2, HID], U8, name="w1_planes", align_bytes=64)
-        nc.vector.memset(w1_planes[:].rearrange("p g n -> p (g n)").bitcast(I32), 0)
-
         warm = const.tile([P, 1], F32, name="warm")
         nc.vector.memset(warm[:], 0.0)
         warm_out = const.tile([P, 1], F32, name="warm_out")
         nc.scalar.activation(out=warm_out[:], in_=warm[:], func=ACT.Gelu)
+
+        def scale_tile(groups, name):
+            planes = const.tile([P, groups, HID], U8, name=name, align_bytes=64)
+            nc.vector.memset(planes[:].rearrange("p g n -> p (g n)").bitcast(I32), 0)
+            return planes
+
+        wz_planes = [scale_tile(CHUNK_GROUPS, "wz_planes%d" % c) for c in range(CHUNKS)]
+        w1_planes = scale_tile(2, "w1_planes")
 
         ident_f32 = const.tile([P, P], F32, name="ident_f32")
         make_identity(nc, ident_f32[:])
         ident_bf16 = const.tile([P, P], BF16, name="ident_bf16")
         make_identity(nc, ident_bf16[:])
 
-        att_raw = const.tile([P, TOKEN_TILES * HID], BF16, name="att_raw")
-        nc.sync.dma_start(
-            out=att_raw[:].rearrange("p (m k) -> p m k", m=TOKEN_TILES),
-            in_=attention_out.rearrange("(m p) k -> p m k", p=P),
-        )
-
         z_raw = {}
         wz_words = {}
         w1_words = const.tile([P, 2, PACK * HID], U8, name="w1_words", align_bytes=64)
 
-        def load_scale_rows(planes, offset, scales):
+        def load_scale_rows(queue, view, planes, scales):
             rows = scales.rearrange("g (q r) n -> r q g n", r=4)
             for r in range(4):
-                nc.sync.dma_start(
-                    out=planes[offset + r : P : 32, :, :].bitcast(I32), in_=rows[r].bitcast(I32)
-                )
+                queue.dma_start(out=planes[r:P:32, :, :].bitcast(view), in_=rows[r].bitcast(view))
+
+        def chunk_groups(c):
+            return slice(c * CHUNK_GROUPS, (c + 1) * CHUNK_GROUPS)
+
+        for c in range(1, CHUNKS):
+            load_scale_rows(nc.gpsimd, F32, wz_planes[c], Wz_scales[chunk_groups(c)])
+        load_scale_rows(nc.gpsimd, F32, w1_planes, w1_deq_scales)
 
         def load_words(words, packed, groups):
             nc.sync.dma_start(
@@ -124,8 +127,9 @@ def tile_synapsemodel_pa_k_kernel(
             )
 
         def load_chunk_weights(c):
-            chunk = slice(c * CHUNK_GROUPS, (c + 1) * CHUNK_GROUPS)
-            load_scale_rows(wz_planes, PACK * c, Wz_scales[chunk])
+            chunk = chunk_groups(c)
+            if c == 0:
+                load_scale_rows(nc.sync, I32, wz_planes[c], Wz_scales[chunk])
             wz_words[c] = const.tile(
                 [P, CHUNK_GROUPS, PACK * HID], U8, name="wz_words%d" % c, align_bytes=64
             )
@@ -148,17 +152,23 @@ def tile_synapsemodel_pa_k_kernel(
                 if first == k - 1:
                     load_chunk_weights(chunk)
                     if chunk == CHUNKS - 1:
-                        load_scale_rows(w1_planes, 0, w1_deq_scales)
                         load_words(w1_words, w1_deq_words, slice(0, 2))
 
-        def transpose_units(raw, units, banks):
-            words = raw[:].bitcast(F32).rearrange("p (a q u) -> p a u q", a=units, u=2)
+        def sort_words(raw, units):
+            in_runs = sorted_pool.tile([P, units, 2, P], F32, name="in_runs")
+            nc.vector.tensor_copy(
+                out=in_runs[:].rearrange("p a u q -> p a q u"),
+                in_=raw[:].bitcast(F32).rearrange("p (a q u) -> p a q u", a=units, u=2),
+            )
+            return in_runs
+
+        def transpose_units(in_runs, units, banks):
             turned = []
             for b in range(units // 2):
                 bank = psum.tile([P, 2, 2, P], F32, name="turned", tag=banks[b])
                 for a in range(2):
                     for u in range(2):
-                        nc.tensor.transpose(bank[:, a, u, :], words[:, 2 * b + a, u, :], ident_f32[:])
+                        nc.tensor.transpose(bank[:, a, u, :], in_runs[:, 2 * b + a, u, :], ident_f32[:])
                 turned.append(bank)
             return turned
 
@@ -180,6 +190,7 @@ def tile_synapsemodel_pa_k_kernel(
                     in_=grouped[:, first * P * PACK : (first + QUANT_GROUPS) * P * PACK],
                 )
 
+        z_runs = {}
         z_turned = {}
         z_grouped = {}
         z_codes = {}
@@ -187,10 +198,12 @@ def tile_synapsemodel_pa_k_kernel(
         sums = {}
         passes_done = {m: 0 for m in range(TOKEN_TILES)}
 
+        def sort_round(k):
+            z_runs[k] = sort_words(z_raw[k], CHUNK_GROUPS)
+
         def transpose_round(k):
-            z_turned[k] = transpose_units(z_raw[k], CHUNK_GROUPS, turn_bank)
+            z_turned[k] = transpose_units(z_runs[k], CHUNK_GROUPS, turn_bank)
             z_grouped[k] = interleave(z_turned[k], CHUNK_GROUPS)
-            load_round(k + Z_BUFS)
 
         def quantise_round(k):
             z_codes[k] = codes_pool.tile([P, CHUNK_GROUPS * P], U32, name="z_codes", align_bytes=64)
@@ -208,17 +221,23 @@ def tile_synapsemodel_pa_k_kernel(
                     lhsT=z_codes[k][:, tokens].bitcast(FP8X4),
                     lhsT_scale=z_planes[k][:, tokens],
                     rhs=wz_words[c][:, g, :].bitcast(FP8X4),
-                    rhs_scale=wz_planes[PACK * c : P, g, :],
+                    rhs_scale=wz_planes[c][:, g, :],
                     start=(passes_done[m] == 0),
                     stop=(passes_done[m] == D_IN // K_PASS - 1),
                 )
                 passes_done[m] += 1
 
-        def norm_head(sums_in, bias, gain, by_word_position):
+        def norm_head(sums_in, bias, gain):
             x = post.tile([P, HID], F32, name="x")
             total = stat.tile([P, 1], F32, name="total")
             nc.vector.scalar_tensor_tensor(
-                out=x[:], in0=sums_in[:], scalar=1.0, in1=bias, op0=ALU.mult, op1=ALU.add, accum_out=total[:]
+                out=x[:].rearrange("p (t q) -> p t q", t=PACK),
+                in0=sums_in,
+                scalar=1.0,
+                in1=bias.rearrange("p (t q) -> p t q", t=PACK),
+                op0=ALU.mult,
+                op1=ALU.add,
+                accum_out=total[:],
             )
             neg_mean = stat.tile([P, 1], F32, name="neg_mean")
             nc.vector.tensor_scalar(
@@ -236,19 +255,8 @@ def tile_synapsemodel_pa_k_kernel(
             rstd = stat.tile([P, 1], F32, name="rstd")
             nc.gpsimd.tensor_tensor(out=rstd[:], in0=var_eps[:], in1=neg_half[:], op=ALU.pow)
             centred = post.tile([P, HID], F32, name="centred")
-            if by_word_position:
-                x_view = x[:].rearrange("p (q t) -> p t q", t=PACK)
-                shape = "p (t q) -> p t q"
-            else:
-                x_view = x[:].rearrange("p (t q) -> p t q", t=PACK)
-                shape = "p (t q) -> p t q"
             nc.vector.scalar_tensor_tensor(
-                out=centred[:].rearrange(shape, t=PACK),
-                in0=x_view,
-                scalar=neg_mean[:],
-                in1=gain.rearrange(shape, t=PACK),
-                op0=ALU.add,
-                op1=ALU.mult,
+                out=centred[:], in0=x[:], scalar=neg_mean[:], in1=gain, op0=ALU.add, op1=ALU.mult
             )
             return centred, rstd
 
@@ -257,33 +265,47 @@ def tile_synapsemodel_pa_k_kernel(
                 out=result, in0=centred[:], scalar=rstd[:], in1=shift, op0=ALU.mult, op1=ALU.add
             )
 
-        for k in range(Z_BUFS):
+        load_round(0)
+        att_raw = const.tile([P, TOKEN_TILES * HID], BF16, name="att_raw")
+        nc.sync.dma_start(
+            out=att_raw[:].rearrange("p (m k) -> p m k", m=TOKEN_TILES),
+            in_=attention_out.rearrange("(m p) k -> p m k", p=P),
+        )
+        for k in range(1, Z_BUFS):
             load_round(k)
 
         spread = const.tile([P, len(vectors), HID], BF16, name="spread")
         for pair in range(len(vectors) // 2):
             both = psum.tile([P, 2, HID], BF16, name="both", tag=sum_bank[pair])
-            for v in range(2):
+            for half in range(2):
                 nc.tensor.matmul(
-                    out=both[:, v, :], lhsT=ones[:], rhs=vector_rows[:, 2 * pair + v, :], start=True, stop=True
+                    out=both[:, half, :],
+                    lhsT=ones[:],
+                    rhs=vector_rows[:, 2 * pair + half, :],
+                    start=True,
+                    stop=True,
                 )
-            if pair < 2:
-                nc.scalar.copy(out=spread[:, 2 * pair : 2 * pair + 2, :], in_=both[:])
-            else:
+            for half in range(2):
+                v = 2 * pair + half
+                in_order = "p (q t) -> p t q" if v < 3 else "p (t q) -> p t q"
                 nc.scalar.copy(
-                    out=spread[:, 2 * pair : 2 * pair + 2, :].rearrange("p v (t q) -> p v t q", t=PACK),
-                    in_=both[:].rearrange("p v (q t) -> p v t q", t=PACK),
+                    out=spread[:, v, :].rearrange("p (t q) -> p t q", t=PACK),
+                    in_=both[:, half, :].rearrange(in_order, t=PACK),
                 )
-        bz_all, b1_all, g1_all, b1_ln_all, gz_all, bz_ln_all = [spread[:, v, :] for v in range(len(vectors))]
+        bz_all, gz_all, bz_ln_all, b1_all, g1_all, b1_ln_all = [spread[:, v, :] for v in range(len(vectors))]
 
-        att_turned = transpose_units(att_raw, TOKEN_TILES, [sum_bank[3], sum_bank[0]])
+        sort_round(0)
+        load_round(Z_BUFS)
+        att_runs = sort_words(att_raw, TOKEN_TILES)
+        sort_round(1)
+        load_round(Z_BUFS + 1)
+        transpose_round(0)
+        att_turned = transpose_units(att_runs, TOKEN_TILES, [sum_bank[3], sum_bank[2]])
         att_grouped = interleave(att_turned, TOKEN_TILES)
         att_codes = const.tile([P, TOKENS], U32, name="att_codes", align_bytes=64)
         att_planes = const.tile([P, TOKENS], U8, name="att_planes", align_bytes=64)
-
-        transpose_round(0)
-        quantise(att_grouped, att_codes, att_planes, TOKEN_TILES)
         quantise_round(0)
+        quantise(att_grouped, att_codes, att_planes, TOKEN_TILES)
 
         centred_1 = {}
         rstd_1 = {}
@@ -297,7 +319,8 @@ def tile_synapsemodel_pa_k_kernel(
         normed = {}
 
         def first_norm_head(m):
-            centred_1[m], rstd_1[m] = norm_head(sums[m], bz_all, gz_all, True)
+            in_word_order = sums[m][:].rearrange("p (q t) -> p t q", t=PACK)
+            centred_1[m], rstd_1[m] = norm_head(in_word_order, bz_all, gz_all)
 
         def first_norm_tail(m):
             z_proj[m] = post.tile([P, PACK, P], BF16, name="z_proj")
@@ -342,7 +365,8 @@ def tile_synapsemodel_pa_k_kernel(
             )
 
         def second_norm_head(m):
-            centred_2[m], rstd_2[m] = norm_head(y_sums[m], b1_all, g1_all, False)
+            as_it_lies = y_sums[m][:].rearrange("p (t q) -> p t q", t=PACK)
+            centred_2[m], rstd_2[m] = norm_head(as_it_lies, b1_all, g1_all)
 
         def second_norm_tail(m):
             normed[m] = post.tile([P, HID], F32, name="normed")
@@ -360,6 +384,9 @@ def tile_synapsemodel_pa_k_kernel(
             ended_2_ago = tile_finished_in.get(k - 2)
             ended_3_ago = tile_finished_in.get(k - 3)
 
+            if k + 2 < N_ROUNDS:
+                sort_round(k + 2)
+                load_round(k + 2 + Z_BUFS)
             if ended_1_ago is not None:
                 first_norm_tail(ended_1_ago)
             if ended_2_ago is not None:

@@ -25,14 +25,11 @@ CHUNK_GROUPS = 8
 CHUNK_K = CHUNK_GROUPS * K_PASS
 CHUNKS = D_IN // CHUNK_K
 QUANT_GROUPS = 4
-Z_BUFS = 5
+Z_BUFS = 4
 
 FLOPS = 2 * TOKENS * D_IN * HID + 2 * TOKENS * (2 * HID) * HID
 
-EARLY_CHUNKS = CHUNKS // 2
-ROUNDS = [(c, m) for c in range(EARLY_CHUNKS) for m in range(TOKEN_TILES)] + [
-    (c, m) for m in range(TOKEN_TILES) for c in range(EARLY_CHUNKS, CHUNKS)
-]
+ROUNDS = [(c, m) for c in range(CHUNKS) for m in range(TOKEN_TILES)]
 N_ROUNDS = len(ROUNDS)
 
 
@@ -69,7 +66,8 @@ def tile_synapsemodel_pa_k_kernel(
         grouped_pool = ctx.enter_context(tc.tile_pool(name="grouped_pool", bufs=2))
         codes_pool = ctx.enter_context(tc.tile_pool(name="codes_pool", bufs=3))
         post = ctx.enter_context(tc.tile_pool(name="post", bufs=2))
-        stat = ctx.enter_context(tc.tile_pool(name="stat", bufs=2))
+        per_tile = ctx.enter_context(tc.tile_pool(name="per_tile", bufs=TOKEN_TILES))
+        stat = ctx.enter_context(tc.tile_pool(name="stat", bufs=TOKEN_TILES))
         psum = ctx.enter_context(tc.psum_pool(name="psum", bufs=1))
         ctx.enter_context(tc.manual_schedule())
 
@@ -149,7 +147,7 @@ def tile_synapsemodel_pa_k_kernel(
                 out=z_raw[k][:], in_=z[m * P : (m + 1) * P, c * CHUNK_K : (c + 1) * CHUNK_K]
             )
             for chunk, first in first_round_of_chunk.items():
-                if first == k - 1:
+                if first == k - 2:
                     load_chunk_weights(chunk)
                     if chunk == CHUNKS - 1:
                         load_words(w1_words, w1_deq_words, slice(0, 2))
@@ -227,7 +225,7 @@ def tile_synapsemodel_pa_k_kernel(
                 )
                 passes_done[m] += 1
 
-        def norm_head(sums_in, bias, gain):
+        def norm_head(sums_in, bias, gain, centred):
             x = post.tile([P, HID], F32, name="x")
             total = stat.tile([P, 1], F32, name="total")
             nc.vector.scalar_tensor_tensor(
@@ -254,11 +252,10 @@ def tile_synapsemodel_pa_k_kernel(
             )
             rstd = stat.tile([P, 1], F32, name="rstd")
             nc.gpsimd.tensor_tensor(out=rstd[:], in0=var_eps[:], in1=neg_half[:], op=ALU.pow)
-            centred = post.tile([P, HID], F32, name="centred")
             nc.vector.scalar_tensor_tensor(
                 out=centred[:], in0=x[:], scalar=neg_mean[:], in1=gain, op0=ALU.add, op1=ALU.mult
             )
-            return centred, rstd
+            return rstd
 
         def norm_tail(centred, rstd, shift, result):
             nc.vector.scalar_tensor_tensor(
@@ -316,11 +313,11 @@ def tile_synapsemodel_pa_k_kernel(
         y_sums = {}
         centred_2 = {}
         rstd_2 = {}
-        normed = {}
 
         def first_norm_head(m):
             in_word_order = sums[m][:].rearrange("p (q t) -> p t q", t=PACK)
-            centred_1[m], rstd_1[m] = norm_head(in_word_order, bz_all, gz_all)
+            centred_1[m] = post.tile([P, HID], F32, name="centred_1")
+            rstd_1[m] = norm_head(in_word_order, bz_all, gz_all, centred_1[m])
 
         def first_norm_tail(m):
             z_proj[m] = post.tile([P, PACK, P], BF16, name="z_proj")
@@ -366,46 +363,44 @@ def tile_synapsemodel_pa_k_kernel(
 
         def second_norm_head(m):
             as_it_lies = y_sums[m][:].rearrange("p (t q) -> p t q", t=PACK)
-            centred_2[m], rstd_2[m] = norm_head(as_it_lies, b1_all, g1_all)
+            centred_2[m] = per_tile.tile([P, HID], F32, name="centred_2")
+            rstd_2[m] = norm_head(as_it_lies, b1_all, g1_all, centred_2[m])
 
         def second_norm_tail(m):
-            normed[m] = post.tile([P, HID], F32, name="normed")
-            norm_tail(centred_2[m], rstd_2[m], b1_ln_all, normed[m][:])
+            norm_tail(centred_2[m], rstd_2[m], b1_ln_all, centred_2[m][:])
 
         def gelu_and_store(m):
-            result = post.tile([P, HID], F32, name="result")
-            nc.scalar.activation(out=result[:], in_=normed[m][:], func=ACT.Gelu)
+            result = per_tile.tile([P, HID], F32, name="result")
+            nc.scalar.activation(out=result[:], in_=centred_2[m][:], func=ACT.Gelu)
             nc.sync.dma_start(out=out[m * P : (m + 1) * P, :], in_=result[:])
 
-        SECOND_STAGE_STEPS = 3
-        for k in range(N_ROUNDS + SECOND_STAGE_STEPS + 1):
-            ended_now = tile_finished_in.get(k)
-            ended_1_ago = tile_finished_in.get(k - 1)
-            ended_2_ago = tile_finished_in.get(k - 2)
-            ended_3_ago = tile_finished_in.get(k - 3)
+        PARTS_IN_STEPS = 5
+        for k in range(N_ROUNDS + PARTS_IN_STEPS):
+            ended = [tile_finished_in.get(k - steps_ago) for steps_ago in range(PARTS_IN_STEPS)]
 
             if k + 2 < N_ROUNDS:
                 sort_round(k + 2)
                 load_round(k + 2 + Z_BUFS)
-            if ended_1_ago is not None:
-                first_norm_tail(ended_1_ago)
-            if ended_2_ago is not None:
-                quantise_z_proj(ended_2_ago)
-            if ended_3_ago is not None:
-                second_norm_tail(ended_3_ago)
+            if ended[4] is not None:
+                second_norm_head(ended[4])
             if k + 1 < N_ROUNDS:
                 transpose_round(k + 1)
-            if ended_3_ago is not None:
-                gelu_and_store(ended_3_ago)
-            if ended_2_ago is not None:
-                second_matmul(ended_2_ago)
-            if k < N_ROUNDS:
-                multiply_round(k)
-            if ended_1_ago is not None:
-                transpose_z_proj(ended_1_ago)
+            if ended[1] is not None:
+                first_norm_tail(ended[1])
             if k + 1 < N_ROUNDS:
                 quantise_round(k + 1)
-            if ended_2_ago is not None:
-                second_norm_head(ended_2_ago)
-            if ended_now is not None:
-                first_norm_head(ended_now)
+            if k < N_ROUNDS:
+                multiply_round(k)
+            if ended[3] is not None:
+                second_matmul(ended[3])
+            if ended[2] is not None:
+                quantise_z_proj(ended[2])
+            if ended[1] is not None:
+                transpose_z_proj(ended[1])
+            if ended[0] is not None:
+                first_norm_head(ended[0])
+
+        for m in range(TOKEN_TILES):
+            second_norm_tail(m)
+        for m in range(TOKEN_TILES):
+            gelu_and_store(m)

@@ -114,9 +114,12 @@ def tile_synapsemodel_pa_k_kernel(
         def chunk_groups(c):
             return slice(c * CHUNK_GROUPS, (c + 1) * CHUNK_GROUPS)
 
-        for c in range(1, CHUNKS):
-            load_scale_rows(nc.gpsimd, F32, wz_planes[c], Wz_scales[chunk_groups(c)])
-        load_scale_rows(nc.gpsimd, F32, w1_planes, w1_deq_scales)
+        def load_later_scale_rows(k):
+            for c in range(1, CHUNKS):
+                if first_round_of_chunk[c - 1] == k:
+                    load_scale_rows(nc.gpsimd, F32, wz_planes[c], Wz_scales[chunk_groups(c)])
+                    if c == CHUNKS - 1:
+                        load_scale_rows(nc.gpsimd, F32, w1_planes, w1_deq_scales)
 
         def load_words(words, packed, groups):
             nc.sync.dma_start(
@@ -381,6 +384,7 @@ def tile_synapsemodel_pa_k_kernel(
             if k + 2 < N_ROUNDS:
                 sort_round(k + 2)
                 load_round(k + 2 + Z_BUFS)
+            load_later_scale_rows(k)
             if ended[4] is not None:
                 second_norm_head(ended[4])
             if k + 1 < N_ROUNDS:

@@ -90,12 +90,15 @@ def tile_synapsemodel_pa_k_kernel(
         nc.scalar.activation(out=warm_out[:], in_=warm[:], func=ACT.Gelu)
 
         def scale_tile(groups, name):
-            planes = const.tile([P, groups, HID], U8, name=name, align_bytes=64)
+            return const.tile([P, groups, HID], U8, name=name, align_bytes=64)
+
+        def zero_planes(planes):
             nc.vector.memset(planes[:].rearrange("p g n -> p (g n)").bitcast(I32), 0)
-            return planes
 
         wz_planes = [scale_tile(CHUNK_GROUPS, "wz_planes%d" % c) for c in range(CHUNKS)]
         w1_planes = scale_tile(2, "w1_planes")
+        zero_planes(wz_planes[0])
+        zero_planes(wz_planes[1])
 
         ident_f32 = const.tile([P, P], F32, name="ident_f32")
         make_identity(nc, ident_f32[:])
@@ -115,11 +118,15 @@ def tile_synapsemodel_pa_k_kernel(
             return slice(c * CHUNK_GROUPS, (c + 1) * CHUNK_GROUPS)
 
         def load_later_scale_rows(k):
-            for c in range(1, CHUNKS):
-                if first_round_of_chunk[c - 1] == k:
+            for c in range(2, CHUNKS):
+                if first_round_of_chunk[c - 2] == k:
+                    zero_planes(wz_planes[c])
                     load_scale_rows(nc.gpsimd, F32, wz_planes[c], Wz_scales[chunk_groups(c)])
                     if c == CHUNKS - 1:
+                        zero_planes(w1_planes)
                         load_scale_rows(nc.gpsimd, F32, w1_planes, w1_deq_scales)
+
+        load_scale_rows(nc.gpsimd, F32, wz_planes[1], Wz_scales[chunk_groups(1)])
 
         def load_words(words, packed, groups):
             nc.sync.dma_start(

@@ -26,6 +26,7 @@ CHUNK_K = CHUNK_GROUPS * K_PASS
 CHUNKS = D_IN // CHUNK_K
 QUANT_GROUPS = 4
 Z_BUFS = 4
+FIRST_RUN = 2
 
 FLOPS = 2 * TOKENS * D_IN * HID + 2 * TOKENS * (2 * HID) * HID
 
@@ -64,7 +65,7 @@ def tile_synapsemodel_pa_k_kernel(
         z_pool = ctx.enter_context(tc.tile_pool(name="z_pool", bufs=Z_BUFS))
         sorted_pool = ctx.enter_context(tc.tile_pool(name="sorted_pool", bufs=3))
         grouped_pool = ctx.enter_context(tc.tile_pool(name="grouped_pool", bufs=2))
-        codes_pool = ctx.enter_context(tc.tile_pool(name="codes_pool", bufs=3))
+        codes_pool = ctx.enter_context(tc.tile_pool(name="codes_pool", bufs=FIRST_RUN + 1))
         post = ctx.enter_context(tc.tile_pool(name="post", bufs=2))
         per_tile = ctx.enter_context(tc.tile_pool(name="per_tile", bufs=TOKEN_TILES))
         stat = ctx.enter_context(tc.tile_pool(name="stat", bufs=TOKEN_TILES))
@@ -157,7 +158,7 @@ def tile_synapsemodel_pa_k_kernel(
                 out=z_raw[k][:], in_=z[m * P : (m + 1) * P, c * CHUNK_K : (c + 1) * CHUNK_K]
             )
             for chunk, first in first_round_of_chunk.items():
-                if first == k - 2:
+                if first == k - (FIRST_RUN if chunk == 0 else 2):
                     load_chunk_weights(chunk)
                     if chunk == CHUNKS - 1:
                         load_words(w1_words, w1_deq_words, slice(0, 2))
@@ -400,7 +401,10 @@ def tile_synapsemodel_pa_k_kernel(
                 first_norm_tail(ended[1])
             if k + 1 < N_ROUNDS:
                 quantise_round(k + 1)
-            if k < N_ROUNDS:
+            if k == FIRST_RUN - 1:
+                for held_back in range(FIRST_RUN - 1):
+                    multiply_round(held_back)
+            if FIRST_RUN - 1 <= k < N_ROUNDS:
                 multiply_round(k)
             if ended[3] is not None:
                 second_matmul(ended[3])

@@ -160,8 +160,8 @@ def tile_synapsemodel_pa_k_kernel(
             for chunk, first in first_round_of_chunk.items():
                 if first == k - (FIRST_RUN if chunk == 0 else 2):
                     load_chunk_weights(chunk)
-                    if chunk == CHUNKS - 1:
-                        load_words(w1_words, w1_deq_words, slice(0, 2))
+            if k == N_ROUNDS - 1:
+                load_words(w1_words, w1_deq_words, slice(0, 2))
 
         def sort_words(raw, units):
             in_runs = sorted_pool.tile([P, units, 2, P], F32, name="in_runs")
@@ -248,18 +248,18 @@ def tile_synapsemodel_pa_k_kernel(
                 op1=ALU.add,
                 accum_out=total[:],
             )
+            squares = post.tile([P, HID], BF16, name="squares")
+            sum_sq = stat.tile([P, 1], F32, name="sum_sq")
+            nc.scalar.activation(
+                out=squares[:], in_=x[:], func=ACT.Square, bias=total[:], scale=-1.0 * HID, accum_out=sum_sq[:]
+            )
             neg_mean = stat.tile([P, 1], F32, name="neg_mean")
             nc.vector.tensor_scalar(
                 out=neg_mean[:], in0=total[:], scalar1=-1.0 / HID, scalar2=None, op0=ALU.mult
             )
-            squares = post.tile([P, HID], BF16, name="squares")
-            sum_sq = stat.tile([P, 1], F32, name="sum_sq")
-            nc.scalar.activation(
-                out=squares[:], in_=x[:], func=ACT.Square, bias=neg_mean[:], scale=1.0, accum_out=sum_sq[:]
-            )
             var_eps = stat.tile([P, 1], F32, name="var_eps")
             nc.gpsimd.tensor_scalar(
-                out=var_eps[:], in0=sum_sq[:], scalar1=1.0 / HID, scalar2=LN_EPS, op0=ALU.mult, op1=ALU.add
+                out=var_eps[:], in0=sum_sq[:], scalar1=1.0 / HID**3, scalar2=LN_EPS, op0=ALU.mult, op1=ALU.add
             )
             rstd = stat.tile([P, 1], F32, name="rstd")
             nc.gpsimd.tensor_tensor(out=rstd[:], in0=var_eps[:], in1=neg_half[:], op=ALU.pow)

from contextlib import ExitStack

import concourse.mybir as mybir
from concourse.masks import make_identity

F32 = mybir.dt.float32
BF16 = mybir.dt.bfloat16
I32 = mybir.dt.int32
U32 = mybir.dt.uint32
U8 = mybir.dt.uint8
FP8X4 = mybir.dt.float8_e4m3fn_x4
ALU = mybir.AluOpType
ACT = mybir.ActivationFunctionType

P = 128
PACK = 4
K_PASS = P * PACK
TOKENS = 512
D_IN = 16384
HID = 512
LN_EPS = 1e-5

TOKEN_TILES = TOKENS // P
CHUNK_GROUPS = 8
CHUNK_K = CHUNK_GROUPS * K_PASS
CHUNKS = D_IN // CHUNK_K
QUANT_GROUPS = 4
Z_BUFS = 4
FIRST_RUN = 2

FLOPS = 2 * TOKENS * D_IN * HID + 2 * TOKENS * (2 * HID) * HID

ROUNDS = [(c, m) for c in range(CHUNKS) for m in range(TOKEN_TILES)]
N_ROUNDS = len(ROUNDS)


def tile_synapsemodel_pa_k_kernel(
    tc,
    z,
    attention_out,
    Wz_words,
    Wz_scales,
    bz,
    gz,
    bz_ln,
    w1_deq_words,
    w1_deq_scales,
    b1,
    g1,
    b1_ln,
    out,
):
    nc = tc.nc

    first_round_of_chunk = {}
    last_round_of_tile = {}
    for k, (c, m) in enumerate(ROUNDS):
        if c not in first_round_of_chunk:
            first_round_of_chunk[c] = k
        last_round_of_tile[m] = k
    tile_finished_in = {k: m for m, k in last_round_of_tile.items()}

    with ExitStack() as ctx:
        const = ctx.enter_context(tc.tile_pool(name="const", bufs=1))
        z_pool = ctx.enter_context(tc.tile_pool(name="z_pool", bufs=Z_BUFS))
        sorted_pool = ctx.enter_context(tc.tile_pool(name="sorted_pool", bufs=3))
        grouped_pool = ctx.enter_context(tc.tile_pool(name="grouped_pool", bufs=2))
        codes_pool = ctx.enter_context(tc.tile_pool(name="codes_pool", bufs=FIRST_RUN + 1))
        post = ctx.enter_context(tc.tile_pool(name="post", bufs=2))
        per_tile = ctx.enter_context(tc.tile_pool(name="per_tile", bufs=TOKEN_TILES))
        stat = ctx.enter_context(tc.tile_pool(name="stat", bufs=TOKEN_TILES))
        psum = ctx.enter_context(tc.psum_pool(name="psum", bufs=1))
        ctx.enter_context(tc.manual_schedule())

        sum_bank = ["sum_bank%d" % m for m in range(TOKEN_TILES)]
        turn_bank = ["turn_bank%d" % b for b in range(CHUNK_GROUPS // 2)]

        vectors = (bz, gz, bz_ln, b1, g1, b1_ln)
        vector_rows = const.tile([P, len(vectors), HID], BF16, name="vector_rows")
        nc.vector.memset(vector_rows[:].rearrange("p v h -> p (v h)").bitcast(I32), 0)
        for v, vector in enumerate(vectors):
            nc.scalar.dma_start(out=vector_rows[0:1, v, :], in_=vector.unsqueeze(0))
        ones = const.tile([P, P], BF16, name="ones")
        nc.vector.memset(ones[:], 1.0)
        neg_half = const.tile([P, 1], F32, name="neg_half")
        nc.vector.memset(neg_half[:], -0.5)

        warm = const.tile([P, 1], F32, name="warm")
        nc.vector.memset(warm[:], 0.0)
        warm_out = const.tile([P, 1], F32, name="warm_out")
        nc.scalar.activation(out=warm_out[:], in_=warm[:], func=ACT.Gelu)

        def scale_tile(groups, name):
            return const.tile([P, groups, HID], U8, name=name, align_bytes=64)

        def zero_planes(planes):
            nc.vector.memset(planes[:].rearrange("p g n -> p (g n)").bitcast(I32), 0)

        wz_planes = [scale_tile(CHUNK_GROUPS, "wz_planes%d" % c) for c in range(CHUNKS)]
        w1_planes = scale_tile(2, "w1_planes")
        zero_planes(wz_planes[0])
        zero_planes(wz_planes[1])

        ident_f32 = const.tile([P, P], F32, name="ident_f32")
        make_identity(nc, ident_f32[:])
        ident_bf16 = const.tile([P, P], BF16, name="ident_bf16")
        make_identity(nc, ident_bf16[:])

        z_raw = {}
        wz_words = {}
        w1_words = const.tile([P, 2, PACK * HID], U8, name="w1_words", align_bytes=64)

        def load_scale_rows(queue, view, planes, scales):
            rows = scales.rearrange("g (q r) n -> r q g n", r=4)
            for r in range(4):
                queue.dma_start(out=planes[r:P:32, :, :].bitcast(view), in_=rows[r].bitcast(view))

        def chunk_groups(c):
            return slice(c * CHUNK_GROUPS, (c + 1) * CHUNK_GROUPS)

        def load_later_scale_rows(k):
            for c in range(2, CHUNKS):
                if first_round_of_chunk[c - 2] == k:
                    zero_planes(wz_planes[c])
                    load_scale_rows(nc.gpsimd, F32, wz_planes[c], Wz_scales[chunk_groups(c)])
                    if c == CHUNKS - 1:
                        zero_planes(w1_planes)
                        load_scale_rows(nc.gpsimd, F32, w1_planes, w1_deq_scales)

        load_scale_rows(nc.gpsimd, F32, wz_planes[1], Wz_scales[chunk_groups(1)])

        def load_words(words, packed, groups):
            nc.sync.dma_start(
                out=words[:, groups, :].bitcast(I32),
                in_=packed[groups].rearrange("g p n t -> p g (n t)").bitcast(I32),
            )

        def load_chunk_weights(c):
            chunk = chunk_groups(c)
            if c == 0:
                load_scale_rows(nc.sync, I32, wz_planes[c], Wz_scales[chunk])
            wz_words[c] = const.tile(
                [P, CHUNK_GROUPS, PACK * HID], U8, name="wz_words%d" % c, align_bytes=64
            )
            for half in range(2):
                load_words(
                    wz_words[c],
                    Wz_words[chunk],
                    slice(half * QUANT_GROUPS, (half + 1) * QUANT_GROUPS),
                )

        def load_round(k):
            if k >= N_ROUNDS:
                return
            c, m = ROUNDS[k]
            z_raw[k] = z_pool.tile([P, CHUNK_K], BF16, name="z_raw")
            nc.sync.dma_start(
                out=z_raw[k][:], in_=z[m * P : (m + 1) * P, c * CHUNK_K : (c + 1) * CHUNK_K]
            )
            for chunk, first in first_round_of_chunk.items():
                if first == k - (FIRST_RUN if chunk == 0 else 2):
                    load_chunk_weights(chunk)
            if k == N_ROUNDS - 1:
                load_words(w1_words, w1_deq_words, slice(0, 2))

        def sort_words(raw, units):
            in_runs = sorted_pool.tile([P, units, 2, P], F32, name="in_runs")
            nc.vector.tensor_copy(
                out=in_runs[:].rearrange("p a u q -> p a q u"),
                in_=raw[:].bitcast(F32).rearrange("p (a q u) -> p a q u", a=units, u=2),
            )
            return in_runs

        def transpose_units(in_runs, units, banks):
            turned = []
            for b in range(units // 2):
                bank = psum.tile([P, 2, 2, P], F32, name="turned", tag=banks[b])
                for a in range(2):
                    for u in range(2):
                        nc.tensor.transpose(bank[:, a, u, :], in_runs[:, 2 * b + a, u, :], ident_f32[:])
                turned.append(bank)
            return turned

        def interleave(turned, units):
            grouped = grouped_pool.tile([P, units * P * PACK], BF16, name="grouped", align_bytes=64)
            pairs = grouped[:].bitcast(F32).rearrange("p (a m u) -> p a m u", a=units, u=2)
            for b, bank in enumerate(turned):
                nc.scalar.copy(
                    out=pairs[:, 2 * b : 2 * b + 2], in_=bank[:].rearrange("p a u m -> p a m u")
                )
            return grouped

        def quantise(grouped, codes, planes, units):
            for first in range(0, units, QUANT_GROUPS):
                cols = slice(first * P, (first + QUANT_GROUPS) * P)
                nc.vector.quantize_mx(
                    out=codes[:, cols].bitcast(FP8X4),
                    scales=planes[:, cols],
                    in_=grouped[:, first * P * PACK : (first + QUANT_GROUPS) * P * PACK],
                )

        z_runs = {}
        z_turned = {}
        z_grouped = {}
        z_codes = {}
        z_planes = {}
        sums = {}
        passes_done = {m: 0 for m in range(TOKEN_TILES)}

        def sort_round(k):
            z_runs[k] = sort_words(z_raw[k], CHUNK_GROUPS)

        def transpose_round(k):
            z_turned[k] = transpose_units(z_runs[k], CHUNK_GROUPS, turn_bank)
            z_grouped[k] = interleave(z_turned[k], CHUNK_GROUPS)

        def quantise_round(k):
            z_codes[k] = codes_pool.tile([P, CHUNK_GROUPS * P], U32, name="z_codes", align_bytes=64)
            z_planes[k] = codes_pool.tile([P, CHUNK_GROUPS * P], U8, name="z_planes", align_bytes=64)
            quantise(z_grouped[k], z_codes[k], z_planes[k], CHUNK_GROUPS)

        def multiply_round(k):
            c, m = ROUNDS[k]
            if passes_done[m] == 0:
                sums[m] = psum.tile([P, HID], F32, name="sums", tag=sum_bank[m])
            for g in range(CHUNK_GROUPS):
                tokens = slice(g * P, (g + 1) * P)
                nc.tensor.matmul_mx(
                    out=sums[m][:],
                    lhsT=z_codes[k][:, tokens].bitcast(FP8X4),
                    lhsT_scale=z_planes[k][:, tokens],
                    rhs=wz_words[c][:, g, :].bitcast(FP8X4),
                    rhs_scale=wz_planes[c][:, g, :],
                    start=(passes_done[m] == 0),
                    stop=(passes_done[m] == D_IN // K_PASS - 1),
                )
                passes_done[m] += 1

        def norm_head(sums_in, bias, gain, centred):
            x = post.tile([P, HID], F32, name="x")
            total = stat.tile([P, 1], F32, name="total")
            nc.vector.scalar_tensor_tensor(
                out=x[:].rearrange("p (t q) -> p t q", t=PACK),
                in0=sums_in,
                scalar=1.0,
                in1=bias.rearrange("p (t q) -> p t q", t=PACK),
                op0=ALU.mult,
                op1=ALU.add,
                accum_out=total[:],
            )
            squares = post.tile([P, HID], BF16, name="squares")
            sum_sq = stat.tile([P, 1], F32, name="sum_sq")
            nc.scalar.activation(
                out=squares[:], in_=x[:], func=ACT.Square, bias=total[:], scale=-1.0 * HID, accum_out=sum_sq[:]
            )
            neg_mean = stat.tile([P, 1], F32, name="neg_mean")
            nc.vector.tensor_scalar(
                out=neg_mean[:], in0=total[:], scalar1=-1.0 / HID, scalar2=None, op0=ALU.mult
            )
            var_eps = stat.tile([P, 1], F32, name="var_eps")
            nc.gpsimd.tensor_scalar(
                out=var_eps[:], in0=sum_sq[:], scalar1=1.0 / HID**3, scalar2=LN_EPS, op0=ALU.mult, op1=ALU.add
            )
            rstd = stat.tile([P, 1], F32, name="rstd")
            nc.gpsimd.tensor_tensor(out=rstd[:], in0=var_eps[:], in1=neg_half[:], op=ALU.pow)
            nc.vector.scalar_tensor_tensor(
                out=centred[:], in0=x[:], scalar=neg_mean[:], in1=gain, op0=ALU.add, op1=ALU.mult
            )
            return rstd

        def norm_tail(centred, rstd, shift, result):
            nc.vector.scalar_tensor_tensor(
                out=result, in0=centred[:], scalar=rstd[:], in1=shift, op0=ALU.mult, op1=ALU.add
            )

        load_round(0)
        att_raw = const.tile([P, TOKEN_TILES * HID], BF16, name="att_raw")
        nc.sync.dma_start(
            out=att_raw[:].rearrange("p (m k) -> p m k", m=TOKEN_TILES),
            in_=attention_out.rearrange("(m p) k -> p m k", p=P),
        )
        for k in range(1, Z_BUFS):
            load_round(k)

        spread = const.tile([P, len(vectors), HID], BF16, name="spread")
        for pair in range(len(vectors) // 2):
            both = psum.tile([P, 2, HID], BF16, name="both", tag=sum_bank[pair])
            for half in range(2):
                nc.tensor.matmul(
                    out=both[:, half, :],
                    lhsT=ones[:],
                    rhs=vector_rows[:, 2 * pair + half, :],
                    start=True,
                    stop=True,
                )
            for half in range(2):
                v = 2 * pair + half
                in_order = "p (q t) -> p t q" if v < 3 else "p (t q) -> p t q"
                nc.scalar.copy(
                    out=spread[:, v, :].rearrange("p (t q) -> p t q", t=PACK),
                    in_=both[:, half, :].rearrange(in_order, t=PACK),
                )
        bz_all, gz_all, bz_ln_all, b1_all, g1_all, b1_ln_all = [spread[:, v, :] for v in range(len(vectors))]

        sort_round(0)
        load_round(Z_BUFS)
        att_runs = sort_words(att_raw, TOKEN_TILES)
        sort_round(1)
        load_round(Z_BUFS + 1)
        transpose_round(0)
        att_turned = transpose_units(att_runs, TOKEN_TILES, [sum_bank[3], sum_bank[2]])
        att_grouped = interleave(att_turned, TOKEN_TILES)
        att_codes = const.tile([P, TOKENS], U32, name="att_codes", align_bytes=64)
        att_planes = const.tile([P, TOKENS], U8, name="att_planes", align_bytes=64)
        quantise_round(0)
        quantise(att_grouped, att_codes, att_planes, TOKEN_TILES)

        centred_1 = {}
        rstd_1 = {}
        z_proj = {}
        zp_grouped = {}
        zp_codes = {}
        zp_planes = {}
        y_sums = {}
        centred_2 = {}
        rstd_2 = {}

        def first_norm_head(m):
            in_word_order = sums[m][:].rearrange("p (q t) -> p t q", t=PACK)
            centred_1[m] = post.tile([P, HID], F32, name="centred_1")
            rstd_1[m] = norm_head(in_word_order, bz_all, gz_all, centred_1[m])

        def first_norm_tail(m):
            z_proj[m] = post.tile([P, PACK, P], BF16, name="z_proj")
            norm_tail(centred_1[m], rstd_1[m], bz_ln_all, z_proj[m][:].rearrange("p t q -> p (t q)"))

        def transpose_z_proj(m):
            turned = psum.tile([P, PACK, P], BF16, name="zp_turned", tag=sum_bank[m])
            for t in range(PACK):
                nc.tensor.transpose(turned[:, t, :], z_proj[m][:, t, :], ident_bf16[:])
            zp_grouped[m] = post.tile([P, P, PACK], BF16, name="zp_grouped", align_bytes=64)
            nc.scalar.copy(out=zp_grouped[m][:], in_=turned[:].rearrange("p t m -> p m t"))

        def quantise_z_proj(m):
            zp_codes[m] = post.tile([P, P], U32, name="zp_codes", align_bytes=64)
            zp_planes[m] = post.tile([P, P], U8, name="zp_planes", align_bytes=64)
            nc.vector.quantize_mx(
                out=zp_codes[m][:].bitcast(FP8X4),
                scales=zp_planes[m][:],
                in_=zp_grouped[m][:].rearrange("p m t -> p (m t)"),
            )

        def second_matmul(m):
            tokens = slice(m * P, (m + 1) * P)
            y_sums[m] = psum.tile([P, HID], F32, name="y_sums", tag=sum_bank[m])
            nc.tensor.matmul_mx(
                out=y_sums[m][:],
                lhsT=att_codes[:, tokens].bitcast(FP8X4),
                lhsT_scale=att_planes[:, tokens],
                rhs=w1_words[:, 1, :].bitcast(FP8X4),
                rhs_scale=w1_planes[:, 1, :],
                start=True,
                stop=False,
            )
            nc.tensor.matmul_mx(
                out=y_sums[m][:],
                lhsT=zp_codes[m][:].bitcast(FP8X4),
                lhsT_scale=zp_planes[m][:],
                rhs=w1_words[:, 0, :].bitcast(FP8X4),
                rhs_scale=w1_planes[:, 0, :],
                start=False,
                stop=True,
            )

        def second_norm_head(m):
            as_it_lies = y_sums[m][:].rearrange("p (t q) -> p t q", t=PACK)
            centred_2[m] = per_tile.tile([P, HID], F32, name="centred_2")
            rstd_2[m] = norm_head(as_it_lies, b1_all, g1_all, centred_2[m])

        def second_norm_tail(m):
            norm_tail(centred_2[m], rstd_2[m], b1_ln_all, centred_2[m][:])

        def gelu_and_store(m):
            result = per_tile.tile([P, HID], F32, name="result")
            nc.scalar.activation(out=result[:], in_=centred_2[m][:], func=ACT.Gelu)
            nc.sync.dma_start(out=out[m * P : (m + 1) * P, :], in_=result[:])

        PARTS_IN_STEPS = 5
        for k in range(N_ROUNDS + PARTS_IN_STEPS):
            ended = [tile_finished_in.get(k - steps_ago) for steps_ago in range(PARTS_IN_STEPS)]

            if k + 2 < N_ROUNDS:
                sort_round(k + 2)
                load_round(k + 2 + Z_BUFS)
            load_later_scale_rows(k)
            if ended[4] is not None:
                second_norm_head(ended[4])
            if k + 1 < N_ROUNDS:
                transpose_round(k + 1)
            if ended[1] is not None:
                first_norm_tail(ended[1])
            if k + 1 < N_ROUNDS:
                quantise_round(k + 1)
            if k == FIRST_RUN - 1:
                for held_back in range(FIRST_RUN - 1):
                    multiply_round(held_back)
            if FIRST_RUN - 1 <= k < N_ROUNDS:
                multiply_round(k)
            if ended[3] is not None:
                second_matmul(ended[3])
            if ended[2] is not None:
                quantise_z_proj(ended[2])
            if ended[1] is not None:
                transpose_z_proj(ended[1])
            if ended[0] is not None:
                first_norm_head(ended[0])

        for m in range(TOKEN_TILES):
            second_norm_tail(m)
        for m in range(TOKEN_TILES):
            gelu_and_store(m)
